import numpy as np
import ml_dtypes


def mxq(x, axis, fmt="e4m3"):
    dtype, down = {"e4m3": (ml_dtypes.float8_e4m3fn, 7), "e5m2": (ml_dtypes.float8_e5m2, 14)}[fmt]
    v = np.moveaxis(np.asarray(x, np.float32).astype(ml_dtypes.bfloat16).astype(np.float64), axis, -1)
    blocks = v.reshape(v.shape[:-1] + (-1, 32))
    amax = np.abs(blocks).max(-1, keepdims=True)
    byte = np.maximum(np.where(amax > 0, np.frexp(amax)[1] - 1 + 127, 0) - down, 1)
    scale = np.exp2(byte - 127.0)
    codes = (blocks / scale).astype(np.float32).astype(dtype).astype(np.float64)
    return np.moveaxis((codes * scale).reshape(v.shape), -1, axis)


WIDE = False


def mx_kscale(k):
    if not WIDE:
        return np.ones(k)
    levels = np.array([10, -10, 5, -5, 0])
    if k % 512:
        return np.exp2(np.random.permutation(np.resize(levels, k // 32))).repeat(32)
    a = np.empty((k // 512, 16))
    for p in range(k // 512):
        a[p, :8] = np.random.permutation(np.resize(levels, 8))
        for g in range(8):
            far = levels[np.abs(levels - a[p, g]) >= 10]
            a[p, g + 8] = far[np.random.randint(len(far))]
    return np.exp2(a.ravel()).repeat(32)


BF16 = ml_dtypes.bfloat16


def bf(x):
    return np.asarray(x, np.float32).astype(BF16)


def f64(x):
    return np.asarray(x).astype(np.float64)


B, S, H, NH, NKV, HD = 1, 512, 2048, 16, 4, 128
HALF = HD // 2
THETA = 10000.0


def rope_tables():
    inv_freq = 1.0 / THETA ** (np.arange(0, HD, 2) / HD)
    freqs = np.arange(S)[:, None] * inv_freq[None, :]
    emb = np.concatenate([freqs, freqs], axis=-1)
    return np.cos(emb), np.sin(emb)


def rotate_half(u):
    return np.concatenate([-u[..., HALF:], u[..., :HALF]], axis=-1)


def heads(y, n):
    return y.reshape(B, S, n, HD).transpose(0, 2, 1, 3)


def draw0():
    s = mx_kscale(H)
    return {"x": bf(np.random.standard_normal((B, S, H)) * s),
            "Wq": bf(np.random.standard_normal((NH * HD, H)) * 1.25 / np.sqrt(H) / s[None, :]),
            "Wk": bf(np.random.standard_normal((NKV * HD, H)) * 1.25 / np.sqrt(H) / s[None, :]),
            "Wv": bf(np.random.standard_normal((NKV * HD, H)) / np.sqrt(H) / s[None, :])}


def core(x, Wq, Wk, Wv):
    xq = mxq(f64(x), 2, "e4m3")
    q = heads(xq @ mxq(f64(Wq), 1, "e4m3").T, NH)
    k = heads(xq @ mxq(f64(Wk), 1, "e4m3").T, NKV)
    v = heads(xq @ mxq(f64(Wv), 1, "e4m3").T, NKV)
    cos, sin = rope_tables()
    q_rot = q * cos + rotate_half(q) * sin
    k_rot = k * cos + rotate_half(k) * sin
    return q_rot, k_rot, v


def e4m3fn_bytes(y):
    return np.clip(np.asarray(y, np.float64), -448.0, 448.0).astype(np.float32).astype(ml_dtypes.float8_e4m3fn).view(np.uint8)


def e4m3fn_values(b):
    return np.asarray(b, np.uint8).view(ml_dtypes.float8_e4m3fn).astype(np.float64)


def setup_inputs():
    d = draw0()
    x0 = np.asarray(d['Wq']).astype(np.float64)
    s = (np.max(np.abs(x0), axis=(0,), keepdims=True) / 448.0).astype(np.float32)
    out = {}
    for k, v in d.items():
        if k == 'Wq':
            out['Wq_bytes'] = e4m3fn_bytes(x0 / s.astype(np.float64))
            out['Wq_scale'] = s
        else:
            out[k] = v
    return out


def reference(x, Wq_bytes, Wq_scale, Wk, Wv):
    return core(x, e4m3fn_values(Wq_bytes) * Wq_scale.astype(np.float64), Wk, Wv)

@@ -1,0 +1,308 @@
+from contextlib import ExitStack
+import math
+
+import concourse.mybir as mybir
+from concourse.masks import make_identity
+
+F32 = mybir.dt.float32
+BF16 = mybir.dt.bfloat16
+U32 = mybir.dt.uint32
+U8 = mybir.dt.uint8
+I32 = mybir.dt.int32
+FP8 = mybir.dt.float8_e4m3fn
+FP8X4 = mybir.dt.float8_e4m3fn_x4
+ALU = mybir.AluOpType
+ACT = mybir.ActivationFunctionType
+
+P = 128
+S = 512
+H = 2048
+HD = 128
+HALF = 64
+NH = 16
+NKV = 4
+THETA = 10000.0
+TT = S // P
+PASSES = H // 512
+UNIT = 512
+RT = UNIT // P
+WORDS = H // 2
+
+FLOPS = 2 * S * H * (NH + 2 * NKV) * HD
+
+V_INTERLEAVES = ()
+S_ROWS = 3
+TWO_PI_HI = 6.28125
+TWO_PI_LO = 2.0 * math.pi - TWO_PI_HI
+
+
+def tile_efficientattention_pa_kernel(tc, x, Wq_bytes, Wq_scale, Wk, Wv, out_0, out_1, out_2):
+    nc = tc.nc
+    x_rows = x.rearrange("b s h -> (b s) h")
+    q_out = out_0.rearrange("b h s d -> (b h) s d")
+    k_out = out_1.rearrange("b h s d -> (b h) s d")
+    v_out = out_2.rearrange("b h s d -> (b h) s d")
+
+    with ExitStack() as ctx:
+        const = ctx.enter_context(tc.tile_pool(name="const", bufs=1))
+        src = ctx.enter_context(tc.tile_pool(name="src", bufs=1))
+        work = ctx.enter_context(tc.tile_pool(name="work", bufs=2))
+        ps_t = ctx.enter_context(tc.psum_pool(name="ps_t", bufs=4))
+        ps_a = ctx.enter_context(tc.psum_pool(name="ps_a", bufs=4))
+        ctx.enter_context(tc.manual_schedule())
+
+        wq_bytes_sb = []
+        for rt in range(NH):
+            wq_bytes_sb.append(src.tile([P, H], U8, name="wq_bytes_%d" % rt))
+        scale_bc = src.tile([P, H], F32, name="scale_bc")
+        scale_col = src.tile([P, PASSES, 4], F32, name="scale_col")
+
+        def load_q(rt):
+            nc.sync.dma_start(out=wq_bytes_sb[rt][:], in_=Wq_bytes[rt * P:(rt + 1) * P, :])
+
+        def load_rows(dram, i):
+            rows = src.tile([P, H], BF16, name="rows", tag="rows", bufs=8)
+            nc.sync.dma_start(out=rows[:], in_=dram[i * P:(i + 1) * P, :])
+            return rows
+
+        load_q(0)
+        scale_row = Wq_scale.rearrange("o k -> (o k)")
+        for c in range(4):
+            nc.sync.dma_start(out=scale_bc[:, c * 512:(c + 1) * 512], in_=scale_row[c * 512:(c + 1) * 512].partition_broadcast(P))
+        for rt in range(1, 4):
+            load_q(rt)
+        x_sb = [load_rows(x_rows, i) for i in range(TT)]
+        for rt in range(4, 8):
+            load_q(rt)
+        wv_sb = [load_rows(Wv, i) for i in range(TT)]
+        nc.sync.dma_start(out=scale_col[:], in_=Wq_scale.rearrange("o (g p t) -> p (o g) t", p=P, t=4))
+        for rt in range(12, 12 + S_ROWS):
+            load_q(rt)
+        for rt in range(8, 12):
+            load_q(rt)
+        for rt in range(12 + S_ROWS, 16):
+            load_q(rt)
+
+        pos_i = const.tile([P, TT], I32, name="pos_i")
+        nc.gpsimd.iota(pos_i[:], pattern=[[P, TT]], base=0, channel_multiplier=1)
+        ident = const.tile([P, P], F32, name="ident")
+        make_identity(nc, ident[:])
+        freq = const.tile([P, HALF], F32, name="freq")
+        nc.vector.memset(freq[:, 0:1], 1.0)
+        for b in range(6):
+            w = 1 << b
+            nc.vector.tensor_scalar(out=freq[:, w:2 * w], in0=freq[:, 0:w], scalar1=THETA ** (-w / HALF),
+                                    scalar2=None, op0=ALU.mult)
+        pos = const.tile([P, TT], F32, name="pos")
+        nc.vector.tensor_copy(out=pos[:], in_=pos_i[:])
+        ang = const.tile([P, 2, TT, HALF], F32, name="ang")
+        tmp = const.tile([P, 2, TT, HALF], F32, name="tmp")
+        turns = const.tile([P, 2, TT, HALF], I32, name="turns")
+        for c in range(2):
+            for i in range(TT):
+                nc.vector.tensor_scalar(out=ang[:, c, i, :], in0=freq[:], scalar1=pos[:, i:i + 1],
+                                        scalar2=None, op0=ALU.mult)
+        for c in range(2):
+            nc.vector.tensor_scalar(out=tmp[:, c], in0=ang[:, c], scalar1=1.0 / (2.0 * math.pi),
+                                    scalar2=(0.25 if c == 0 else 0.0), op0=ALU.mult, op1=ALU.add)
+        nc.vector.tensor_copy(out=turns[:], in_=tmp[:])
+        nc.vector.tensor_copy(out=tmp[:], in_=turns[:])
+        nc.vector.scalar_tensor_tensor(out=ang[:], in0=tmp[:], scalar=-TWO_PI_HI, in1=ang[:],
+                                       op0=ALU.mult, op1=ALU.add)
+        nc.vector.scalar_tensor_tensor(out=ang[:], in0=tmp[:], scalar=-TWO_PI_LO, in1=ang[:],
+                                       op0=ALU.mult, op1=ALU.add)
+        nc.vector.tensor_scalar(out=ang[:, 0], in0=ang[:, 0], scalar1=math.pi / 2.0, scalar2=None, op0=ALU.add)
+        nc.vector.tensor_scalar(out=tmp[:], in0=ang[:], scalar1=math.pi, scalar2=None, op0=ALU.is_gt)
+        nc.vector.scalar_tensor_tensor(out=ang[:], in0=tmp[:], scalar=-2.0 * math.pi, in1=ang[:],
+                                       op0=ALU.mult, op1=ALU.add)
+        cos2 = const.tile([P, TT, HD], F32, name="cos2")
+        sin_rot = const.tile([P, TT, 2, HALF], F32, name="sin_rot")
+        nc.scalar.activation(out=cos2[:, :, 0:HALF], in_=ang[:, 0], func=ACT.Sin)
+        nc.scalar.activation(out=cos2[:, :, HALF:HD], in_=ang[:, 0], func=ACT.Sin)
+        nc.scalar.activation(out=sin_rot[:, :, 0, :], in_=ang[:, 1], func=ACT.Sin, scale=-1.0)
+        nc.scalar.activation(out=sin_rot[:, :, 1, :], in_=ang[:, 1], func=ACT.Sin)
+
+        x_codes = const.tile([P, TT, UNIT], U32, name="x_codes", align_bytes=64)
+        x_scales = const.tile([P, TT, UNIT], U8, name="x_scales", align_bytes=64)
+
+        def widen(rt, pieces=1):
+            wb = work.tile([P, H], BF16, name="wb", tag="wb", bufs=5)
+            w = H // pieces
+            for c in range(pieces):
+                nc.vector.tensor_tensor(out=wb[:, c * w:(c + 1) * w], in0=wq_bytes_sb[rt][:, c * w:(c + 1) * w].bitcast(FP8),
+                                        in1=scale_bc[:, c * w:(c + 1) * w], op=ALU.mult)
+            return wb
+
+        def new_grouped():
+            return work.tile([P, 4, UNIT, 2], F32, name="grouped", tag="grouped", bufs=3, align_bytes=64)
+
+        def transpose_rows(rows_bf16, dst_of_pair):
+            words = rows_bf16[:].bitcast(F32)
+            for gp in range(2):
+                tb = ps_t.tile([P, 2, 2, P], F32, name="tb", tag="tb", bufs=4)
+                for gg in range(2):
+                    g = 2 * gp + gg
+                    for u in range(2):
+                        nc.tensor.transpose(tb[:, gg, u, :], words[:, 256 * g + u:256 * (g + 1):2], ident[:])
+                nc.scalar.copy(out=dst_of_pair(gp), in_=tb[:].rearrange("p g u r -> p g r u"))
+
+        def transpose_x(grouped, i):
+            transpose_rows(x_sb[i], lambda gp: grouped[:, i, 256 * gp:256 * (gp + 1), :].rearrange(
+                "p (g r) u -> p g r u", g=2))
+
+        def transpose_w(grouped, rows_bf16, rt):
+            transpose_rows(rows_bf16, lambda gp: grouped[:, 2 * gp:2 * gp + 2, rt * P:(rt + 1) * P, :])
+
+        def cast_rows(rt):
+            rows = src.tile([P, H], BF16, name="rows", tag="rows", bufs=8)
+            nc.scalar.copy(out=rows[:], in_=wq_bytes_sb[rt][:].bitcast(FP8))
+            return rows
+
+        def scaled_planes(casts, planes, g, u):
+            tb = ps_t.tile([P, S_ROWS * P], F32, name="tb", tag="tb", bufs=4)
+            for rt in range(S_ROWS):
+                nc.tensor.transpose(tb[:, rt * P:(rt + 1) * P], casts[rt][:].bitcast(F32)[:, 256 * g + u:256 * (g + 1):2],
+                                    ident[:])
+            halves = tb[:].bitcast(BF16).rearrange("p (n e) -> p n e", e=2)
+            for e in range(2):
+                t = 2 * u + e
+                nc.scalar.activation(out=planes[:, g, t, :], in_=halves[:, :, e], func=ACT.Copy,
+                                     scale=scale_col[:, g, t:t + 1])
+
+        def interleave(planes, grouped, g, on_vector):
+            dst = grouped[:, g, 0:S_ROWS * P, :].rearrange("p n u -> p (n u)").bitcast(BF16).rearrange("p (n t) -> p n t", t=4)
+            if on_vector:
+                nc.vector.tensor_copy(out=dst, in_=planes[:, g].rearrange("p t n -> p n t"))
+            else:
+                nc.scalar.copy(out=dst, in_=planes[:, g].rearrange("p t n -> p n t"))
+
+        def quantize(grouped, codes, scales):
+            for a in range(2):
+                nc.vector.quantize_mx(
+                    out=codes[:, 2 * a:2 * a + 2, :].rearrange("p g n -> p (g n)").bitcast(FP8X4),
+                    scales=scales[:, 2 * a:2 * a + 2, :].rearrange("p g n -> p (g n)"),
+                    in_=grouped[:, 2 * a:2 * a + 2].rearrange("p g n u -> p (g n u)").bitcast(BF16),
+                )
+
+        def quantize_unit(grouped):
+            codes = work.tile([P, PASSES, UNIT], U32, name="w_codes", tag="w_codes", bufs=2, align_bytes=64)
+            scales = work.tile([P, PASSES, UNIT], U8, name="w_scales", tag="w_scales", bufs=2, align_bytes=64)
+            quantize(grouped, codes, scales)
+            return codes, scales
+
+        def project_tile(unit_codes, i):
+            codes, scales = unit_codes
+            acc = ps_a.tile([P, 4, HD], F32, name="acc", tag="acc", bufs=4)
+            for g in range(PASSES):
+                nc.tensor.matmul_mx(
+                    out=acc[:].rearrange("p h d -> p (h d)"),
+                    lhsT=x_codes[:, i, g * P:(g + 1) * P].bitcast(FP8X4),
+                    lhsT_scale=x_scales[:, i, g * P:(g + 1) * P],
+                    rhs=codes[:, g, :].bitcast(FP8X4),
+                    rhs_scale=scales[:, g, :],
+                    start=(g == 0),
+                    stop=(g == PASSES - 1),
+                )
+            return acc
+
+        def cos_product(acc, i):
+            ta = work.tile([P, 4, HD], F32, name="ta", tag="ta", bufs=6)
+            nc.vector.tensor_tensor(out=ta[:], in0=acc[:], in1=cos2[:, i:i + 1, :].to_broadcast([P, 4, HD]), op=ALU.mult)
+            return ta
+
+        def sin_product(acc, i):
+            ts = work.tile([P, 4, HD], F32, name="ts", tag="ts", bufs=4)
+            nc.vector.tensor_tensor(out=ts[:].rearrange("p h (c j) -> p h c j", c=2),
+                                    in0=acc[:].rearrange("p h (c j) -> p h c j", c=2)[:, :, ::-1, :],
+                                    in1=sin_rot[:, i:i + 1, :, :].to_broadcast([P, 4, 2, HALF]), op=ALU.mult)
+            return ts
+
+        def add_and_store(engine, ta, ts, dram, i):
+            engine.tensor_tensor(out=ta[:], in0=ta[:], in1=ts[:], op=ALU.add)
+            nc.sync.dma_start(out=dram[:, i * P:(i + 1) * P, :].rearrange("h p d -> p h d"), in_=ta[:])
+
+        def rope(unit_codes, accs, dram, carried, last):
+            if carried is not None:
+                acc3, ta3, dram3 = carried
+                add_and_store(nc.gpsimd, ta3, sin_product(acc3, 3), dram3, 3)
+            if len(accs) < TT:
+                accs = accs + [project_tile(unit_codes, 3)]
+            kept = None
+            for i in range(3):
+                ta = cos_product(accs[i], i)
+                ts = sin_product(accs[i], i)
+                if i < 2:
+                    add_and_store(nc.gpsimd, ta, ts, dram, i)
+                else:
+                    kept = (ta, ts)
+            ta3 = cos_product(accs[3], 3)
+            if last:
+                ts3 = sin_product(accs[3], 3)
+                add_and_store(nc.vector, kept[0], kept[1], dram, 2)
+                add_and_store(nc.vector, ta3, ts3, dram, 3)
+                return None
+            add_and_store(nc.vector, kept[0], kept[1], dram, 2)
+            return (accs[3], ta3, dram)
+
+        def copy_out(accs, dram):
+            for i in range(TT):
+                vt = work.tile([P, 4, HD], F32, name="vt", tag="vt", bufs=4)
+                nc.scalar.copy(out=vt[:], in_=accs[i][:])
+                nc.scalar.dma_start(out=dram[:, i * P:(i + 1) * P, :].rearrange("h p d -> p h d"), in_=vt[:])
+
+        wide0 = [widen(rt, 4 if rt == 0 else 1) for rt in range(RT)]
+        g_x = new_grouped()
+        for i in range(TT):
+            transpose_x(g_x, i)
+        g_q0 = new_grouped()
+        for rt in range(RT):
+            transpose_w(g_q0, wide0[rt], rt)
+        wk_sb = [load_rows(Wk, i) for i in range(TT)]
+        quantize(g_x, x_codes, x_scales)
+        g_v = new_grouped()
+        for rt in range(RT):
+            transpose_w(g_v, wv_sb[rt], rt)
+        g_q1 = new_grouped()
+        casts = []
+        for rt in range(RT):
+            transpose_w(g_q1, widen(4 + rt), rt)
+            if rt < S_ROWS:
+                casts.append(cast_rows(12 + rt))
+        c_v = quantize_unit(g_v)
+        c_q0 = quantize_unit(g_q0)
+        copy_out([project_tile(c_v, i) for i in range(TT)], v_out)
+        g_q2 = new_grouped()
+        planes = work.tile([P, PASSES, 4, S_ROWS * P], BF16, name="planes", tag="planes", bufs=1)
+        for rt in range(1):
+            transpose_w(g_q2, widen(8 + rt), rt)
+        a_q0 = [project_tile(c_q0, i) for i in range(TT)]
+        for rt in range(1, RT):
+            transpose_w(g_q2, widen(8 + rt), rt)
+        wide3 = [widen(12 + rt) for rt in range(S_ROWS, RT)]
+        c_q1 = quantize_unit(g_q1)
+        g_q3 = new_grouped()
+        for rt in range(S_ROWS, RT):
+            transpose_w(g_q3, wide3[rt - S_ROWS], rt)
+        g_k = new_grouped()
+        for rt in range(RT):
+            transpose_w(g_k, wk_sb[rt], rt)
+        carried = rope(c_q0, a_q0, q_out[0:4], None, False)
+        a_q1 = []
+        for i in range(3):
+            a_q1.append(project_tile(c_q1, i))
+            scaled_planes(casts, planes, i, 0)
+            scaled_planes(casts, planes, i, 1)
+        c_q2 = quantize_unit(g_q2)
+        carried = rope(c_q1, a_q1, q_out[4:8], carried, False)
+        scaled_planes(casts, planes, 3, 0)
+        scaled_planes(casts, planes, 3, 1)
+        a_q2 = [project_tile(c_q2, i) for i in range(3)]
+        for g in range(PASSES):
+            interleave(planes, g_q3, g, g in V_INTERLEAVES)
+        c_k = quantize_unit(g_k)
+        carried = rope(c_q2, a_q2, q_out[8:12], carried, False)
+        a_k = [project_tile(c_k, i) for i in range(3)]
+        c_q3 = quantize_unit(g_q3)
+        carried = rope(c_k, a_k, k_out, carried, False)
+        a_q3 = [project_tile(c_q3, i) for i in range(3)]
+        rope(c_q3, a_q3, q_out[12:16], carried, True)

@@ -66,9 +66,7 @@ def tile_efficientattention_pa_kernel(tc, x, Wq_bytes, Wq_scale, Wk, Wv, out_0, 
             return rows
 
         load_q(0)
-        scale_row = Wq_scale.rearrange("o k -> (o k)")
-        for c in range(4):
-            nc.sync.dma_start(out=scale_bc[:, c * 512:(c + 1) * 512], in_=scale_row[c * 512:(c + 1) * 512].partition_broadcast(P))
+        nc.sync.dma_start(out=scale_bc[:], in_=Wq_scale.rearrange("o k -> (o k)").partition_broadcast(P))
         for rt in range(1, 4):
             load_q(rt)
         x_sb = [load_rows(x_rows, i) for i in range(TT)]
@@ -250,7 +248,7 @@ def tile_efficientattention_pa_kernel(tc, x, Wq_bytes, Wq_scale, Wk, Wv, out_0, 
                 nc.scalar.copy(out=vt[:], in_=accs[i][:])
                 nc.scalar.dma_start(out=dram[:, i * P:(i + 1) * P, :].rearrange("h p d -> p h d"), in_=vt[:])
 
-        wide0 = [widen(rt, 4 if rt == 0 else 1) for rt in range(RT)]
+        wide0 = [widen(rt) for rt in range(RT)]
         g_x = new_grouped()
         for i in range(TT):
             transpose_x(g_x, i)

@@ -290,13 +290,15 @@ def tile_efficientattention_pa_kernel(tc, x, Wq_bytes, Wq_scale, Wk, Wv, out_0, 
             a_q1.append(project_tile(c_q1, i))
             scaled_planes(casts, planes, i, 0)
             scaled_planes(casts, planes, i, 1)
+            if i > 0:
+                interleave(planes, g_q3, i - 1, False)
         c_q2 = quantize_unit(g_q2)
         carried = rope(c_q1, a_q1, q_out[4:8], carried, False)
         scaled_planes(casts, planes, 3, 0)
         scaled_planes(casts, planes, 3, 1)
         a_q2 = [project_tile(c_q2, i) for i in range(3)]
-        for g in range(PASSES):
-            interleave(planes, g_q3, g, g in V_INTERLEAVES)
+        for g in range(2, PASSES):
+            interleave(planes, g_q3, g, False)
         c_k = quantize_unit(g_k)
         carried = rope(c_q2, a_q2, q_out[8:12], carried, False)
         a_k = [project_tile(c_k, i) for i in range(3)]

@@ -256,6 +256,7 @@ def tile_efficientattention_pa_kernel(tc, x, Wq_bytes, Wq_scale, Wk, Wv, out_0, 
         for rt in range(RT):
             transpose_w(g_q0, wide0[rt], rt)
         wk_sb = [load_rows(Wk, i) for i in range(TT)]
+        wide1 = [widen(4 + rt) for rt in range(2)]
         quantize(g_x, x_codes, x_scales)
         g_v = new_grouped()
         for rt in range(RT):
@@ -263,7 +264,7 @@ def tile_efficientattention_pa_kernel(tc, x, Wq_bytes, Wq_scale, Wk, Wv, out_0, 
         g_q1 = new_grouped()
         casts = []
         for rt in range(RT):
-            transpose_w(g_q1, widen(4 + rt), rt)
+            transpose_w(g_q1, wide1[rt] if rt < 2 else widen(4 + rt), rt)
             if rt < S_ROWS:
                 casts.append(cast_rows(12 + rt))
         c_v = quantize_unit(g_v)

@@ -8,7 +8,6 @@ F32 = mybir.dt.float32
 BF16 = mybir.dt.bfloat16
 U32 = mybir.dt.uint32
 U8 = mybir.dt.uint8
-I32 = mybir.dt.int32
 FP8 = mybir.dt.float8_e4m3fn
 FP8X4 = mybir.dt.float8_e4m3fn_x4
 ALU = mybir.AluOpType
@@ -30,10 +29,7 @@ WORDS = H // 2
 
 FLOPS = 2 * S * H * (NH + 2 * NKV) * HD
 
-V_INTERLEAVES = ()
 S_ROWS = 3
-TWO_PI_HI = 6.28125
-TWO_PI_LO = 2.0 * math.pi - TWO_PI_HI
 
 
 def tile_efficientattention_pa_kernel(tc, x, Wq_bytes, Wq_scale, Wk, Wv, out_0, out_1, out_2):
@@ -81,44 +77,31 @@ def tile_efficientattention_pa_kernel(tc, x, Wq_bytes, Wq_scale, Wk, Wv, out_0, 
         for rt in range(12 + S_ROWS, 16):
             load_q(rt)
 
-        pos_i = const.tile([P, TT], I32, name="pos_i")
-        nc.gpsimd.iota(pos_i[:], pattern=[[P, TT]], base=0, channel_multiplier=1)
         ident = const.tile([P, P], F32, name="ident")
         make_identity(nc, ident[:])
+        pos = const.tile([P, TT], F32, name="pos")
+        nc.gpsimd.iota(pos[:], pattern=[[P, TT]], base=0, channel_multiplier=1, allow_small_or_imprecise_dtypes=True)
         freq = const.tile([P, HALF], F32, name="freq")
-        nc.vector.memset(freq[:, 0:1], 1.0)
+        nc.gpsimd.memset(freq[:, 0:1], 1.0)
         for b in range(6):
             w = 1 << b
-            nc.vector.tensor_scalar(out=freq[:, w:2 * w], in0=freq[:, 0:w], scalar1=THETA ** (-w / HALF),
-                                    scalar2=None, op0=ALU.mult)
-        pos = const.tile([P, TT], F32, name="pos")
-        nc.vector.tensor_copy(out=pos[:], in_=pos_i[:])
+            nc.gpsimd.tensor_scalar(out=freq[:, w:2 * w], in0=freq[:, 0:w], scalar1=THETA ** (-w / HALF),
+                                    scalar2=1.0, op0=ALU.mult, op1=ALU.mult)
         ang = const.tile([P, 2, TT, HALF], F32, name="ang")
-        tmp = const.tile([P, 2, TT, HALF], F32, name="tmp")
-        turns = const.tile([P, 2, TT, HALF], I32, name="turns")
-        for c in range(2):
-            for i in range(TT):
-                nc.vector.tensor_scalar(out=ang[:, c, i, :], in0=freq[:], scalar1=pos[:, i:i + 1],
-                                        scalar2=None, op0=ALU.mult)
-        for c in range(2):
-            nc.vector.tensor_scalar(out=tmp[:, c], in0=ang[:, c], scalar1=1.0 / (2.0 * math.pi),
-                                    scalar2=(0.25 if c == 0 else 0.0), op0=ALU.mult, op1=ALU.add)
-        nc.vector.tensor_copy(out=turns[:], in_=tmp[:])
-        nc.vector.tensor_copy(out=tmp[:], in_=turns[:])
-        nc.vector.scalar_tensor_tensor(out=ang[:], in0=tmp[:], scalar=-TWO_PI_HI, in1=ang[:],
-                                       op0=ALU.mult, op1=ALU.add)
-        nc.vector.scalar_tensor_tensor(out=ang[:], in0=tmp[:], scalar=-TWO_PI_LO, in1=ang[:],
-                                       op0=ALU.mult, op1=ALU.add)
-        nc.vector.tensor_scalar(out=ang[:, 0], in0=ang[:, 0], scalar1=math.pi / 2.0, scalar2=None, op0=ALU.add)
-        nc.vector.tensor_scalar(out=tmp[:], in0=ang[:], scalar1=math.pi, scalar2=None, op0=ALU.is_gt)
-        nc.vector.scalar_tensor_tensor(out=ang[:], in0=tmp[:], scalar=-2.0 * math.pi, in1=ang[:],
-                                       op0=ALU.mult, op1=ALU.add)
-        cos2 = const.tile([P, TT, HD], F32, name="cos2")
+        turns = const.tile([P, 2, TT, HALF], U32, name="turns")
+        whole = const.tile([P, 2, TT, HALF], F32, name="whole")
+        for i in range(TT):
+            nc.gpsimd.tensor_scalar(out=ang[:, 0, i, :], in0=freq[:], scalar1=pos[:, i:i + 1],
+                                    scalar2=1.0 / (2.0 * math.pi), op0=ALU.mult, op1=ALU.mult)
+        nc.gpsimd.tensor_scalar(out=ang[:, 1], in0=ang[:, 0], scalar1=1.0, scalar2=0.25, op0=ALU.mult, op1=ALU.add)
+        nc.scalar.copy(out=turns[:], in_=ang[:])
+        nc.scalar.activation(out=whole[:], in_=turns[:], func=ACT.Copy)
+        nc.gpsimd.tensor_tensor(out=ang[:], in0=ang[:], in1=whole[:], op=ALU.subtract)
+        cos1 = const.tile([P, TT, HALF], F32, name="cos1")
         sin_rot = const.tile([P, TT, 2, HALF], F32, name="sin_rot")
-        nc.scalar.activation(out=cos2[:, :, 0:HALF], in_=ang[:, 0], func=ACT.Sin)
-        nc.scalar.activation(out=cos2[:, :, HALF:HD], in_=ang[:, 0], func=ACT.Sin)
-        nc.scalar.activation(out=sin_rot[:, :, 0, :], in_=ang[:, 1], func=ACT.Sin, scale=-1.0)
-        nc.scalar.activation(out=sin_rot[:, :, 1, :], in_=ang[:, 1], func=ACT.Sin)
+        nc.scalar.activation(out=cos1[:], in_=ang[:, 1], func=ACT.Sin, scale=2.0 * math.pi)
+        nc.scalar.activation(out=sin_rot[:, :, 0, :], in_=ang[:, 0], func=ACT.Sin, scale=-2.0 * math.pi)
+        nc.scalar.activation(out=sin_rot[:, :, 1, :], in_=ang[:, 0], func=ACT.Sin, scale=2.0 * math.pi)
 
         x_codes = const.tile([P, TT, UNIT], U32, name="x_codes", align_bytes=64)
         x_scales = const.tile([P, TT, UNIT], U8, name="x_scales", align_bytes=64)
@@ -205,7 +188,9 @@ def tile_efficientattention_pa_kernel(tc, x, Wq_bytes, Wq_scale, Wk, Wv, out_0, 
 
         def cos_product(acc, i):
             ta = work.tile([P, 4, HD], F32, name="ta", tag="ta", bufs=6)
-            nc.vector.tensor_tensor(out=ta[:], in0=acc[:], in1=cos2[:, i:i + 1, :].to_broadcast([P, 4, HD]), op=ALU.mult)
+            nc.vector.tensor_tensor(out=ta[:].rearrange("p h (c j) -> p (h c) j", c=2),
+                                    in0=acc[:].rearrange("p h (c j) -> p (h c) j", c=2),
+                                    in1=cos1[:, i:i + 1, :].to_broadcast([P, 8, HALF]), op=ALU.mult)
             return ta
 
         def sin_product(acc, i):

@@ -8,6 +8,7 @@ F32 = mybir.dt.float32
 BF16 = mybir.dt.bfloat16
 U32 = mybir.dt.uint32
 U8 = mybir.dt.uint8
+I32 = mybir.dt.int32
 FP8 = mybir.dt.float8_e4m3fn
 FP8X4 = mybir.dt.float8_e4m3fn_x4
 ALU = mybir.AluOpType
@@ -77,26 +78,26 @@ def tile_efficientattention_pa_kernel(tc, x, Wq_bytes, Wq_scale, Wk, Wv, out_0, 
         for rt in range(12 + S_ROWS, 16):
             load_q(rt)
 
-        ident = const.tile([P, P], F32, name="ident")
-        make_identity(nc, ident[:])
         pos = const.tile([P, TT], F32, name="pos")
         nc.gpsimd.iota(pos[:], pattern=[[P, TT]], base=0, channel_multiplier=1, allow_small_or_imprecise_dtypes=True)
+        ident = const.tile([P, P], F32, name="ident")
+        make_identity(nc, ident[:])
         freq = const.tile([P, HALF], F32, name="freq")
-        nc.gpsimd.memset(freq[:, 0:1], 1.0)
+        nc.vector.memset(freq[:, 0:1], 1.0)
         for b in range(6):
             w = 1 << b
-            nc.gpsimd.tensor_scalar(out=freq[:, w:2 * w], in0=freq[:, 0:w], scalar1=THETA ** (-w / HALF),
-                                    scalar2=1.0, op0=ALU.mult, op1=ALU.mult)
+            nc.vector.tensor_scalar(out=freq[:, w:2 * w], in0=freq[:, 0:w], scalar1=THETA ** (-w / HALF),
+                                    scalar2=None, op0=ALU.mult)
         ang = const.tile([P, 2, TT, HALF], F32, name="ang")
-        turns = const.tile([P, 2, TT, HALF], U32, name="turns")
+        turns = const.tile([P, 2, TT, HALF], I32, name="turns")
         whole = const.tile([P, 2, TT, HALF], F32, name="whole")
         for i in range(TT):
-            nc.gpsimd.tensor_scalar(out=ang[:, 0, i, :], in0=freq[:], scalar1=pos[:, i:i + 1],
+            nc.vector.tensor_scalar(out=ang[:, 0, i, :], in0=freq[:], scalar1=pos[:, i:i + 1],
                                     scalar2=1.0 / (2.0 * math.pi), op0=ALU.mult, op1=ALU.mult)
-        nc.gpsimd.tensor_scalar(out=ang[:, 1], in0=ang[:, 0], scalar1=1.0, scalar2=0.25, op0=ALU.mult, op1=ALU.add)
-        nc.scalar.copy(out=turns[:], in_=ang[:])
-        nc.scalar.activation(out=whole[:], in_=turns[:], func=ACT.Copy)
-        nc.gpsimd.tensor_tensor(out=ang[:], in0=ang[:], in1=whole[:], op=ALU.subtract)
+        nc.vector.tensor_scalar(out=ang[:, 1], in0=ang[:, 0], scalar1=0.25, scalar2=None, op0=ALU.add)
+        nc.vector.tensor_copy(out=turns[:], in_=ang[:])
+        nc.vector.tensor_copy(out=whole[:], in_=turns[:])
+        nc.vector.tensor_tensor(out=ang[:], in0=ang[:], in1=whole[:], op=ALU.subtract)
         cos1 = const.tile([P, TT, HALF], F32, name="cos1")
         sin_rot = const.tile([P, TT, 2, HALF], F32, name="sin_rot")
         nc.scalar.activation(out=cos1[:], in_=ang[:, 1], func=ACT.Sin, scale=2.0 * math.pi)

@@ -30,7 +30,8 @@ WORDS = H // 2
 
 FLOPS = 2 * S * H * (NH + 2 * NKV) * HD
 
-S_ROWS = 3
+S_ROWS = 4
+ROWS_BUFS = 10
 
 
 def tile_efficientattention_pa_kernel(tc, x, Wq_bytes, Wq_scale, Wk, Wv, out_0, out_1, out_2):
@@ -58,39 +59,44 @@ def tile_efficientattention_pa_kernel(tc, x, Wq_bytes, Wq_scale, Wk, Wv, out_0, 
             nc.sync.dma_start(out=wq_bytes_sb[rt][:], in_=Wq_bytes[rt * P:(rt + 1) * P, :])
 
         def load_rows(dram, i):
-            rows = src.tile([P, H], BF16, name="rows", tag="rows", bufs=8)
+            rows = src.tile([P, H], BF16, name="rows", tag="rows", bufs=ROWS_BUFS)
             nc.sync.dma_start(out=rows[:], in_=dram[i * P:(i + 1) * P, :])
             return rows
 
-        load_q(0)
-        nc.sync.dma_start(out=scale_bc[:], in_=Wq_scale.rearrange("o k -> (o k)").partition_broadcast(P))
-        for rt in range(1, 4):
+        for rt in range(0, 4):
             load_q(rt)
-        x_sb = [load_rows(x_rows, i) for i in range(TT)]
-        for rt in range(4, 8):
-            load_q(rt)
-        wv_sb = [load_rows(Wv, i) for i in range(TT)]
         nc.sync.dma_start(out=scale_col[:], in_=Wq_scale.rearrange("o (g p t) -> p (o g) t", p=P, t=4))
-        for rt in range(12, 12 + S_ROWS):
+        for rt in range(12, 14):
             load_q(rt)
-        for rt in range(8, 12):
+        nc.sync.dma_start(out=scale_bc[:], in_=Wq_scale.rearrange("o k -> (o k)").partition_broadcast(P))
+        for rt in range(4, 6):
             load_q(rt)
-        for rt in range(12 + S_ROWS, 16):
+        early = []
+        for rt in range(RT):
+            rows = src.tile([P, H], BF16, name="rows", tag="rows", bufs=ROWS_BUFS)
+            early.append(rows)
+        x_sb = [load_rows(x_rows, i) for i in range(TT)]
+        for rt in range(6, 8):
             load_q(rt)
 
         pos = const.tile([P, TT], F32, name="pos")
         nc.gpsimd.iota(pos[:], pattern=[[P, TT]], base=0, channel_multiplier=1, allow_small_or_imprecise_dtypes=True)
         ident = const.tile([P, P], F32, name="ident")
         make_identity(nc, ident[:])
+        casts = []
+        for rt in range(12, 14):
+            rows = src.tile([P, H], BF16, name="cast_%d" % rt)
+            nc.gpsimd.tensor_copy(out=rows[:], in_=wq_bytes_sb[rt][:].bitcast(FP8))
+            casts.append(rows)
         freq = const.tile([P, HALF], F32, name="freq")
         nc.vector.memset(freq[:, 0:1], 1.0)
         for b in range(6):
             w = 1 << b
             nc.vector.tensor_scalar(out=freq[:, w:2 * w], in0=freq[:, 0:w], scalar1=THETA ** (-w / HALF),
                                     scalar2=None, op0=ALU.mult)
-        ang = const.tile([P, 2, TT, HALF], F32, name="ang")
-        turns = const.tile([P, 2, TT, HALF], I32, name="turns")
-        whole = const.tile([P, 2, TT, HALF], F32, name="whole")
+        ang = work.tile([P, 2, TT, HALF], F32, name="ang", tag="ta", bufs=6)
+        turns = work.tile([P, 2, TT, HALF], I32, name="turns", tag="ta", bufs=6)
+        whole = work.tile([P, 2, TT, HALF], F32, name="whole", tag="ta", bufs=6)
         for i in range(TT):
             nc.vector.tensor_scalar(out=ang[:, 0, i, :], in0=freq[:], scalar1=pos[:, i:i + 1],
                                     scalar2=1.0 / (2.0 * math.pi), op0=ALU.mult, op1=ALU.mult)
@@ -100,9 +106,6 @@ def tile_efficientattention_pa_kernel(tc, x, Wq_bytes, Wq_scale, Wk, Wv, out_0, 
         nc.vector.tensor_tensor(out=ang[:], in0=ang[:], in1=whole[:], op=ALU.subtract)
         cos1 = const.tile([P, TT, HALF], F32, name="cos1")
         sin_rot = const.tile([P, TT, 2, HALF], F32, name="sin_rot")
-        nc.scalar.activation(out=cos1[:], in_=ang[:, 1], func=ACT.Sin, scale=2.0 * math.pi)
-        nc.scalar.activation(out=sin_rot[:, :, 0, :], in_=ang[:, 0], func=ACT.Sin, scale=-2.0 * math.pi)
-        nc.scalar.activation(out=sin_rot[:, :, 1, :], in_=ang[:, 0], func=ACT.Sin, scale=2.0 * math.pi)
 
         x_codes = const.tile([P, TT, UNIT], U32, name="x_codes", align_bytes=64)
         x_scales = const.tile([P, TT, UNIT], U8, name="x_scales", align_bytes=64)
@@ -136,11 +139,35 @@ def tile_efficientattention_pa_kernel(tc, x, Wq_bytes, Wq_scale, Wk, Wv, out_0, 
             transpose_rows(rows_bf16, lambda gp: grouped[:, 2 * gp:2 * gp + 2, rt * P:(rt + 1) * P, :])
 
         def cast_rows(rt):
-            rows = src.tile([P, H], BF16, name="rows", tag="rows", bufs=8)
+            rows = src.tile([P, H], BF16, name="rows", tag="rows", bufs=ROWS_BUFS)
             nc.scalar.copy(out=rows[:], in_=wq_bytes_sb[rt][:].bitcast(FP8))
             return rows
 
-        def scaled_planes(casts, planes, g, u):
+        def cast_early(rt, pieces):
+            n = H // pieces
+            for c in range(pieces):
+                nc.scalar.copy(out=early[rt][:, c * n:(c + 1) * n], in_=wq_bytes_sb[rt][:, c * n:(c + 1) * n].bitcast(FP8))
+
+        def transpose_product(grouped, rows_bf16, rt):
+            words = rows_bf16[:].bitcast(F32)
+            for gp in range(2):
+                tb = ps_t.tile([P, 2, 2, P], F32, name="tb", tag="tb", bufs=4)
+                for gg in range(2):
+                    g = 2 * gp + gg
+                    for u in range(2):
+                        nc.tensor.transpose(tb[:, gg, u, :], words[:, 256 * g + u:256 * (g + 1):2], ident[:])
+                for gg in range(2):
+                    g = 2 * gp + gg
+                    nc.vector.tensor_tensor(
+                        out=grouped[:, g, rt * P:(rt + 1) * P, :].rearrange("p r u -> p (r u)").bitcast(BF16).rearrange("p (r u e) -> p r u e", u=2, e=2),
+                        in0=tb[:, gg].rearrange("p u r -> p (u r)").bitcast(BF16).rearrange("p (u r e) -> p r u e", u=2, e=2),
+                        in1=scale_col[:, g:g + 1, :].to_broadcast([P, P, 4]).rearrange("p r (u e) -> p r u e", u=2),
+                        op=ALU.mult)
+
+        def new_planes():
+            return work.tile([P, 4, UNIT], BF16, name="planes", tag="planes", bufs=2)
+
+        def scaled_planes(planes, g, u):
             tb = ps_t.tile([P, S_ROWS * P], F32, name="tb", tag="tb", bufs=4)
             for rt in range(S_ROWS):
                 nc.tensor.transpose(tb[:, rt * P:(rt + 1) * P], casts[rt][:].bitcast(F32)[:, 256 * g + u:256 * (g + 1):2],
@@ -148,15 +175,18 @@ def tile_efficientattention_pa_kernel(tc, x, Wq_bytes, Wq_scale, Wk, Wv, out_0, 
             halves = tb[:].bitcast(BF16).rearrange("p (n e) -> p n e", e=2)
             for e in range(2):
                 t = 2 * u + e
-                nc.scalar.activation(out=planes[:, g, t, :], in_=halves[:, :, e], func=ACT.Copy,
+                nc.scalar.activation(out=planes[:, t, :], in_=halves[:, :, e], func=ACT.Copy,
                                      scale=scale_col[:, g, t:t + 1])
 
-        def interleave(planes, grouped, g, on_vector):
-            dst = grouped[:, g, 0:S_ROWS * P, :].rearrange("p n u -> p (n u)").bitcast(BF16).rearrange("p (n t) -> p n t", t=4)
-            if on_vector:
-                nc.vector.tensor_copy(out=dst, in_=planes[:, g].rearrange("p t n -> p n t"))
-            else:
-                nc.scalar.copy(out=dst, in_=planes[:, g].rearrange("p t n -> p n t"))
+        def interleave(planes, grouped, g):
+            dst = grouped[:, g].rearrange("p n u -> p (n u)").bitcast(BF16).rearrange("p (n t) -> p n t", t=4)
+            nc.scalar.copy(out=dst, in_=planes[:].rearrange("p t n -> p n t"))
+
+        def scaled_pass(grouped, g):
+            planes = new_planes()
+            scaled_planes(planes, g, 0)
+            scaled_planes(planes, g, 1)
+            return planes
 
         def quantize(grouped, codes, scales):
             for a in range(2):
@@ -166,15 +196,18 @@ def tile_efficientattention_pa_kernel(tc, x, Wq_bytes, Wq_scale, Wk, Wv, out_0, 
                     in_=grouped[:, 2 * a:2 * a + 2].rearrange("p g n u -> p (g n u)").bitcast(BF16),
                 )
 
+        v_codes = const.tile([P, PASSES, UNIT], U32, name="v_codes", align_bytes=64)
+        v_scales = const.tile([P, PASSES, UNIT], U8, name="v_scales", align_bytes=64)
+
         def quantize_unit(grouped):
             codes = work.tile([P, PASSES, UNIT], U32, name="w_codes", tag="w_codes", bufs=2, align_bytes=64)
             scales = work.tile([P, PASSES, UNIT], U8, name="w_scales", tag="w_scales", bufs=2, align_bytes=64)
             quantize(grouped, codes, scales)
             return codes, scales
 
-        def project_tile(unit_codes, i):
+        def project_tile(unit_codes, i, pool=None, tag="acc"):
             codes, scales = unit_codes
-            acc = ps_a.tile([P, 4, HD], F32, name="acc", tag="acc", bufs=4)
+            acc = (pool or ps_a).tile([P, 4, HD], F32, name="acc", tag=tag, bufs=4)
             for g in range(PASSES):
                 nc.tensor.matmul_mx(
                     out=acc[:].rearrange("p h d -> p (h d)"),
@@ -205,12 +238,11 @@ def tile_efficientattention_pa_kernel(tc, x, Wq_bytes, Wq_scale, Wk, Wv, out_0, 
             engine.tensor_tensor(out=ta[:], in0=ta[:], in1=ts[:], op=ALU.add)
             nc.sync.dma_start(out=dram[:, i * P:(i + 1) * P, :].rearrange("h p d -> p h d"), in_=ta[:])
 
-        def rope(unit_codes, accs, dram, carried, last):
-            if carried is not None:
-                acc3, ta3, dram3 = carried
-                add_and_store(nc.gpsimd, ta3, sin_product(acc3, 3), dram3, 3)
-            if len(accs) < TT:
-                accs = accs + [project_tile(unit_codes, 3)]
+        def finish(carried):
+            acc3, ta3, dram3 = carried
+            add_and_store(nc.gpsimd, ta3, sin_product(acc3, 3), dram3, 3)
+
+        def rope(accs, dram, last=False):
             kept = None
             for i in range(3):
                 ta = cos_product(accs[i], i)
@@ -230,66 +262,81 @@ def tile_efficientattention_pa_kernel(tc, x, Wq_bytes, Wq_scale, Wk, Wv, out_0, 
 
         def copy_out(accs, dram):
             for i in range(TT):
-                vt = work.tile([P, 4, HD], F32, name="vt", tag="vt", bufs=4)
+                vt = work.tile([P, 4, HD], F32, name="vt", tag="vt", bufs=3)
                 nc.scalar.copy(out=vt[:], in_=accs[i][:])
                 nc.scalar.dma_start(out=dram[:, i * P:(i + 1) * P, :].rearrange("h p d -> p h d"), in_=vt[:])
 
-        wide0 = [widen(rt) for rt in range(RT)]
+        for rt in range(RT):
+            cast_early(rt, 2)
+        nc.scalar.activation(out=cos1[:], in_=ang[:, 1], func=ACT.Sin, scale=2.0 * math.pi)
+        nc.scalar.activation(out=sin_rot[:, :, 0, :], in_=ang[:, 0], func=ACT.Sin, scale=-2.0 * math.pi)
+        nc.scalar.activation(out=sin_rot[:, :, 1, :], in_=ang[:, 0], func=ACT.Sin, scale=2.0 * math.pi)
         g_x = new_grouped()
-        for i in range(TT):
-            transpose_x(g_x, i)
         g_q0 = new_grouped()
         for rt in range(RT):
-            transpose_w(g_q0, wide0[rt], rt)
-        wk_sb = [load_rows(Wk, i) for i in range(TT)]
+            transpose_product(g_q0, early[rt], rt)
+        for i in range(TT):
+            transpose_x(g_x, i)
+        wv_sb = [load_rows(Wv, i) for i in range(TT)]
+        for rt in range(14, 16):
+            load_q(rt)
+        for rt in range(8, 12):
+            load_q(rt)
         wide1 = [widen(4 + rt) for rt in range(2)]
         quantize(g_x, x_codes, x_scales)
         g_v = new_grouped()
         for rt in range(RT):
             transpose_w(g_v, wv_sb[rt], rt)
+        wk_sb = [load_rows(Wk, i) for i in range(TT)]
         g_q1 = new_grouped()
-        casts = []
         for rt in range(RT):
             transpose_w(g_q1, wide1[rt] if rt < 2 else widen(4 + rt), rt)
-            if rt < S_ROWS:
-                casts.append(cast_rows(12 + rt))
-        c_v = quantize_unit(g_v)
+            if rt < 2:
+                casts.append(cast_rows(14 + rt))
+        quantize(g_v, v_codes, v_scales)
         c_q0 = quantize_unit(g_q0)
-        copy_out([project_tile(c_v, i) for i in range(TT)], v_out)
         g_q2 = new_grouped()
-        planes = work.tile([P, PASSES, 4, S_ROWS * P], BF16, name="planes", tag="planes", bufs=1)
-        for rt in range(1):
-            transpose_w(g_q2, widen(8 + rt), rt)
-        a_q0 = [project_tile(c_q0, i) for i in range(TT)]
-        for rt in range(1, RT):
-            transpose_w(g_q2, widen(8 + rt), rt)
-        wide3 = [widen(12 + rt) for rt in range(S_ROWS, RT)]
-        c_q1 = quantize_unit(g_q1)
         g_q3 = new_grouped()
-        for rt in range(S_ROWS, RT):
-            transpose_w(g_q3, wide3[rt - S_ROWS], rt)
+        planes0 = scaled_pass(g_q3, 0)
+        transpose_w(g_q2, widen(8), 0)
+        interleave(planes0, g_q3, 0)
+        a_q0 = [project_tile(c_q0, i) for i in range(TT)]
+        transpose_w(g_q2, widen(9), 1)
+        planes1 = scaled_pass(g_q3, 1)
+        transpose_w(g_q2, widen(10), 2)
+        interleave(planes1, g_q3, 1)
+        transpose_w(g_q2, widen(11), 3)
+        c_q1 = quantize_unit(g_q1)
         g_k = new_grouped()
-        for rt in range(RT):
-            transpose_w(g_k, wk_sb[rt], rt)
-        carried = rope(c_q0, a_q0, q_out[0:4], None, False)
+        transpose_w(g_k, wk_sb[0], 0)
+        carried = rope(a_q0, q_out[0:4])
         a_q1 = []
         for i in range(3):
             a_q1.append(project_tile(c_q1, i))
-            scaled_planes(casts, planes, i, 0)
-            scaled_planes(casts, planes, i, 1)
-            if i > 0:
-                interleave(planes, g_q3, i - 1, False)
+            if i < 2:
+                transpose_w(g_k, wk_sb[i + 1], i + 1)
         c_q2 = quantize_unit(g_q2)
-        carried = rope(c_q1, a_q1, q_out[4:8], carried, False)
-        scaled_planes(casts, planes, 3, 0)
-        scaled_planes(casts, planes, 3, 1)
+        finish(carried)
+        a_q1.append(project_tile(c_q1, 3))
+        transpose_w(g_k, wk_sb[3], 3)
+        planes2 = scaled_pass(g_q3, 2)
+        carried = rope(a_q1, q_out[4:8])
+        planes3 = scaled_pass(g_q3, 3)
+        interleave(planes2, g_q3, 2)
+        interleave(planes3, g_q3, 3)
         a_q2 = [project_tile(c_q2, i) for i in range(3)]
-        for g in range(2, PASSES):
-            interleave(planes, g_q3, g, False)
         c_k = quantize_unit(g_k)
-        carried = rope(c_q2, a_q2, q_out[8:12], carried, False)
+        finish(carried)
+        a_q2.append(project_tile(c_q2, 3))
+        carried = rope(a_q2, q_out[8:12])
         a_k = [project_tile(c_k, i) for i in range(3)]
+        a_v = [project_tile((v_codes, v_scales), i, ps_t, "tb") for i in range(TT)]
         c_q3 = quantize_unit(g_q3)
-        carried = rope(c_k, a_k, k_out, carried, False)
+        finish(carried)
+        a_k.append(project_tile(c_k, 3))
+        carried = rope(a_k, k_out)
         a_q3 = [project_tile(c_q3, i) for i in range(3)]
-        rope(c_q3, a_q3, q_out[12:16], carried, True)
+        copy_out(a_v, v_out)
+        finish(carried)
+        a_q3.append(project_tile(c_q3, 3))
+        rope(a_q3, q_out[12:16], last=True)

@@ -302,10 +302,9 @@ def tile_efficientattention_pa_kernel(tc, x, Wq_bytes, Wq_scale, Wk, Wv, out_0, 
         interleave(planes0, g_q3, 0)
         a_q0 = [project_tile(c_q0, i) for i in range(TT)]
         transpose_w(g_q2, widen(9), 1)
-        planes1 = scaled_pass(g_q3, 1)
         transpose_w(g_q2, widen(10), 2)
-        interleave(planes1, g_q3, 1)
         transpose_w(g_q2, widen(11), 3)
+        planes1 = scaled_pass(g_q3, 1)
         c_q1 = quantize_unit(g_q1)
         g_k = new_grouped()
         transpose_w(g_k, wk_sb[0], 0)
@@ -313,12 +312,11 @@ def tile_efficientattention_pa_kernel(tc, x, Wq_bytes, Wq_scale, Wk, Wv, out_0, 
         a_q1 = []
         for i in range(3):
             a_q1.append(project_tile(c_q1, i))
-            if i < 2:
-                transpose_w(g_k, wk_sb[i + 1], i + 1)
+            transpose_w(g_k, wk_sb[i + 1], i + 1)
         c_q2 = quantize_unit(g_q2)
         finish(carried)
         a_q1.append(project_tile(c_q1, 3))
-        transpose_w(g_k, wk_sb[3], 3)
+        interleave(planes1, g_q3, 1)
         planes2 = scaled_pass(g_q3, 2)
         carried = rope(a_q1, q_out[4:8])
         planes3 = scaled_pass(g_q3, 3)
@@ -330,11 +328,11 @@ def tile_efficientattention_pa_kernel(tc, x, Wq_bytes, Wq_scale, Wk, Wv, out_0, 
         a_q2.append(project_tile(c_q2, 3))
         carried = rope(a_q2, q_out[8:12])
         a_k = [project_tile(c_k, i) for i in range(3)]
-        a_v = [project_tile((v_codes, v_scales), i, ps_t, "tb") for i in range(TT)]
-        c_q3 = quantize_unit(g_q3)
         finish(carried)
         a_k.append(project_tile(c_k, 3))
+        a_v = [project_tile((v_codes, v_scales), i, ps_t, "tb") for i in range(TT)]
         carried = rope(a_k, k_out)
+        c_q3 = quantize_unit(g_q3)
         a_q3 = [project_tile(c_q3, i) for i in range(3)]
         copy_out(a_v, v_out)
         finish(carried)

@@ -63,9 +63,10 @@ def tile_efficientattention_pa_kernel(tc, x, Wq_bytes, Wq_scale, Wk, Wv, out_0, 
             nc.sync.dma_start(out=rows[:], in_=dram[i * P:(i + 1) * P, :])
             return rows
 
-        for rt in range(0, 4):
-            load_q(rt)
+        load_q(0)
         nc.sync.dma_start(out=scale_col[:], in_=Wq_scale.rearrange("o (g p t) -> p (o g) t", p=P, t=4))
+        for rt in range(1, 4):
+            load_q(rt)
         for rt in range(12, 14):
             load_q(rt)
         nc.sync.dma_start(out=scale_bc[:], in_=Wq_scale.rearrange("o k -> (o k)").partition_broadcast(P))
@@ -83,27 +84,23 @@ def tile_efficientattention_pa_kernel(tc, x, Wq_bytes, Wq_scale, Wk, Wv, out_0, 
         nc.gpsimd.iota(pos[:], pattern=[[P, TT]], base=0, channel_multiplier=1, allow_small_or_imprecise_dtypes=True)
         ident = const.tile([P, P], F32, name="ident")
         make_identity(nc, ident[:])
+        ang = work.tile([P, 2, TT, HALF], F32, name="ang", tag="ta", bufs=6)
+        turns = work.tile([P, 2, TT, HALF], I32, name="turns", tag="ta", bufs=6)
+        whole = work.tile([P, 2, TT, HALF], F32, name="whole", tag="ta", bufs=6)
+        nc.vector.tensor_scalar(out=ang[:, 0, :, 0], in0=pos[:], scalar1=1.0 / (2.0 * math.pi), scalar2=None, op0=ALU.mult)
+        for b in range(6):
+            w = 1 << b
+            nc.vector.tensor_scalar(out=ang[:, 0, :, w:2 * w], in0=ang[:, 0, :, 0:w], scalar1=THETA ** (-w / HALF),
+                                    scalar2=None, op0=ALU.mult)
+        nc.vector.tensor_scalar(out=ang[:, 1], in0=ang[:, 0], scalar1=0.25, scalar2=None, op0=ALU.add)
+        nc.vector.tensor_copy(out=turns[:], in_=ang[:])
+        nc.vector.tensor_copy(out=whole[:], in_=turns[:])
+        nc.gpsimd.tensor_tensor(out=ang[:], in0=ang[:], in1=whole[:], op=ALU.subtract)
         casts = []
         for rt in range(12, 14):
             rows = src.tile([P, H], BF16, name="cast_%d" % rt)
             nc.gpsimd.tensor_copy(out=rows[:], in_=wq_bytes_sb[rt][:].bitcast(FP8))
             casts.append(rows)
-        freq = const.tile([P, HALF], F32, name="freq")
-        nc.vector.memset(freq[:, 0:1], 1.0)
-        for b in range(6):
-            w = 1 << b
-            nc.vector.tensor_scalar(out=freq[:, w:2 * w], in0=freq[:, 0:w], scalar1=THETA ** (-w / HALF),
-                                    scalar2=None, op0=ALU.mult)
-        ang = work.tile([P, 2, TT, HALF], F32, name="ang", tag="ta", bufs=6)
-        turns = work.tile([P, 2, TT, HALF], I32, name="turns", tag="ta", bufs=6)
-        whole = work.tile([P, 2, TT, HALF], F32, name="whole", tag="ta", bufs=6)
-        for i in range(TT):
-            nc.vector.tensor_scalar(out=ang[:, 0, i, :], in0=freq[:], scalar1=pos[:, i:i + 1],
-                                    scalar2=1.0 / (2.0 * math.pi), op0=ALU.mult, op1=ALU.mult)
-        nc.vector.tensor_scalar(out=ang[:, 1], in0=ang[:, 0], scalar1=0.25, scalar2=None, op0=ALU.add)
-        nc.vector.tensor_copy(out=turns[:], in_=ang[:])
-        nc.vector.tensor_copy(out=whole[:], in_=turns[:])
-        nc.vector.tensor_tensor(out=ang[:], in0=ang[:], in1=whole[:], op=ALU.subtract)
         cos1 = const.tile([P, TT, HALF], F32, name="cos1")
         sin_rot = const.tile([P, TT, 2, HALF], F32, name="sin_rot")
 
@@ -255,7 +252,9 @@ def tile_efficientattention_pa_kernel(tc, x, Wq_bytes, Wq_scale, Wk, Wv, out_0, 
             if last:
                 ts3 = sin_product(accs[3], 3)
                 add_and_store(nc.vector, kept[0], kept[1], dram, 2)
-                add_and_store(nc.vector, ta3, ts3, dram, 3)
+                for h in range(0, 4, 2):
+                    nc.vector.tensor_tensor(out=ta3[:, h:h + 2], in0=ta3[:, h:h + 2], in1=ts3[:, h:h + 2], op=ALU.add)
+                    nc.sync.dma_start(out=dram[h:h + 2, 3 * P:4 * P, :].rearrange("h p d -> p h d"), in_=ta3[:, h:h + 2])
                 return None
             add_and_store(nc.vector, kept[0], kept[1], dram, 2)
             return (accs[3], ta3, dram)
@@ -267,7 +266,7 @@ def tile_efficientattention_pa_kernel(tc, x, Wq_bytes, Wq_scale, Wk, Wv, out_0, 
                 nc.scalar.dma_start(out=dram[:, i * P:(i + 1) * P, :].rearrange("h p d -> p h d"), in_=vt[:])
 
         for rt in range(RT):
-            cast_early(rt, 2)
+            cast_early(rt, 4)
         nc.scalar.activation(out=cos1[:], in_=ang[:, 1], func=ACT.Sin, scale=2.0 * math.pi)
         nc.scalar.activation(out=sin_rot[:, :, 0, :], in_=ang[:, 0], func=ACT.Sin, scale=-2.0 * math.pi)
         nc.scalar.activation(out=sin_rot[:, :, 1, :], in_=ang[:, 0], func=ACT.Sin, scale=2.0 * math.pi)
@@ -287,35 +286,38 @@ def tile_efficientattention_pa_kernel(tc, x, Wq_bytes, Wq_scale, Wk, Wv, out_0, 
         g_v = new_grouped()
         for rt in range(RT):
             transpose_w(g_v, wv_sb[rt], rt)
+        c_q0 = quantize_unit(g_q0)
+        a_q0 = [project_tile(c_q0, i) for i in range(TT)]
         wk_sb = [load_rows(Wk, i) for i in range(TT)]
+        for rt in range(2):
+            casts.append(cast_rows(14 + rt))
         g_q1 = new_grouped()
         for rt in range(RT):
             transpose_w(g_q1, wide1[rt] if rt < 2 else widen(4 + rt), rt)
-            if rt < 2:
-                casts.append(cast_rows(14 + rt))
         quantize(g_v, v_codes, v_scales)
-        c_q0 = quantize_unit(g_q0)
         g_q2 = new_grouped()
         g_q3 = new_grouped()
         planes0 = scaled_pass(g_q3, 0)
         transpose_w(g_q2, widen(8), 0)
-        interleave(planes0, g_q3, 0)
-        a_q0 = [project_tile(c_q0, i) for i in range(TT)]
         transpose_w(g_q2, widen(9), 1)
         transpose_w(g_q2, widen(10), 2)
         transpose_w(g_q2, widen(11), 3)
-        planes1 = scaled_pass(g_q3, 1)
         c_q1 = quantize_unit(g_q1)
         g_k = new_grouped()
-        transpose_w(g_k, wk_sb[0], 0)
         carried = rope(a_q0, q_out[0:4])
         a_q1 = []
-        for i in range(3):
-            a_q1.append(project_tile(c_q1, i))
-            transpose_w(g_k, wk_sb[i + 1], i + 1)
+        transpose_w(g_k, wk_sb[0], 0)
+        transpose_w(g_k, wk_sb[1], 1)
+        transpose_w(g_k, wk_sb[2], 2)
+        transpose_w(g_k, wk_sb[3], 3)
+        planes1 = scaled_pass(g_q3, 1)
+        a_q1.append(project_tile(c_q1, 0))
+        a_q1.append(project_tile(c_q1, 1))
+        a_q1.append(project_tile(c_q1, 2))
         c_q2 = quantize_unit(g_q2)
         finish(carried)
         a_q1.append(project_tile(c_q1, 3))
+        interleave(planes0, g_q3, 0)
         interleave(planes1, g_q3, 1)
         planes2 = scaled_pass(g_q3, 2)
         carried = rope(a_q1, q_out[4:8])
@@ -327,10 +329,11 @@ def tile_efficientattention_pa_kernel(tc, x, Wq_bytes, Wq_scale, Wk, Wv, out_0, 
         finish(carried)
         a_q2.append(project_tile(c_q2, 3))
         carried = rope(a_q2, q_out[8:12])
+        a_v = [project_tile((v_codes, v_scales), i, ps_t, "tb") for i in range(1)]
         a_k = [project_tile(c_k, i) for i in range(3)]
         finish(carried)
         a_k.append(project_tile(c_k, 3))
-        a_v = [project_tile((v_codes, v_scales), i, ps_t, "tb") for i in range(TT)]
+        a_v += [project_tile((v_codes, v_scales), i, ps_t, "tb") for i in range(1, TT)]
         carried = rope(a_k, k_out)
         c_q3 = quantize_unit(g_q3)
         a_q3 = [project_tile(c_q3, i) for i in range(3)]

@@ -63,9 +63,8 @@ def tile_efficientattention_pa_kernel(tc, x, Wq_bytes, Wq_scale, Wk, Wv, out_0, 
             nc.sync.dma_start(out=rows[:], in_=dram[i * P:(i + 1) * P, :])
             return rows
 
-        load_q(0)
-        nc.sync.dma_start(out=scale_col[:], in_=Wq_scale.rearrange("o (g p t) -> p (o g) t", p=P, t=4))
-        for rt in range(1, 4):
+        nc.scalar.dma_start(out=scale_col[:], in_=Wq_scale.rearrange("o (g p t) -> p (o g) t", p=P, t=4))
+        for rt in range(0, 4):
             load_q(rt)
         for rt in range(12, 14):
             load_q(rt)
@@ -84,6 +83,11 @@ def tile_efficientattention_pa_kernel(tc, x, Wq_bytes, Wq_scale, Wk, Wv, out_0, 
         nc.gpsimd.iota(pos[:], pattern=[[P, TT]], base=0, channel_multiplier=1, allow_small_or_imprecise_dtypes=True)
         ident = const.tile([P, P], F32, name="ident")
         make_identity(nc, ident[:])
+        casts = []
+        for rt in range(12, 14):
+            rows = src.tile([P, H], BF16, name="cast_%d" % rt)
+            nc.gpsimd.tensor_copy(out=rows[:], in_=wq_bytes_sb[rt][:].bitcast(FP8))
+            casts.append(rows)
         ang = work.tile([P, 2, TT, HALF], F32, name="ang", tag="ta", bufs=6)
         turns = work.tile([P, 2, TT, HALF], I32, name="turns", tag="ta", bufs=6)
         whole = work.tile([P, 2, TT, HALF], F32, name="whole", tag="ta", bufs=6)
@@ -95,12 +99,7 @@ def tile_efficientattention_pa_kernel(tc, x, Wq_bytes, Wq_scale, Wk, Wv, out_0, 
         nc.vector.tensor_scalar(out=ang[:, 1], in0=ang[:, 0], scalar1=0.25, scalar2=None, op0=ALU.add)
         nc.vector.tensor_copy(out=turns[:], in_=ang[:])
         nc.vector.tensor_copy(out=whole[:], in_=turns[:])
-        nc.gpsimd.tensor_tensor(out=ang[:], in0=ang[:], in1=whole[:], op=ALU.subtract)
-        casts = []
-        for rt in range(12, 14):
-            rows = src.tile([P, H], BF16, name="cast_%d" % rt)
-            nc.gpsimd.tensor_copy(out=rows[:], in_=wq_bytes_sb[rt][:].bitcast(FP8))
-            casts.append(rows)
+        nc.vector.tensor_tensor(out=ang[:], in0=ang[:], in1=whole[:], op=ALU.subtract)
         cos1 = const.tile([P, TT, HALF], F32, name="cos1")
         sin_rot = const.tile([P, TT, 2, HALF], F32, name="sin_rot")
 
@@ -266,7 +265,7 @@ def tile_efficientattention_pa_kernel(tc, x, Wq_bytes, Wq_scale, Wk, Wv, out_0, 
                 nc.scalar.dma_start(out=dram[:, i * P:(i + 1) * P, :].rearrange("h p d -> p h d"), in_=vt[:])
 
         for rt in range(RT):
-            cast_early(rt, 4)
+            cast_early(rt, 2)
         nc.scalar.activation(out=cos1[:], in_=ang[:, 1], func=ACT.Sin, scale=2.0 * math.pi)
         nc.scalar.activation(out=sin_rot[:, :, 0, :], in_=ang[:, 0], func=ACT.Sin, scale=-2.0 * math.pi)
         nc.scalar.activation(out=sin_rot[:, :, 1, :], in_=ang[:, 0], func=ACT.Sin, scale=2.0 * math.pi)

from contextlib import ExitStack
import math

import concourse.mybir as mybir
from concourse.masks import make_identity

F32 = mybir.dt.float32
BF16 = mybir.dt.bfloat16
U32 = mybir.dt.uint32
U8 = mybir.dt.uint8
I32 = mybir.dt.int32
FP8 = mybir.dt.float8_e4m3fn
FP8X4 = mybir.dt.float8_e4m3fn_x4
ALU = mybir.AluOpType
ACT = mybir.ActivationFunctionType

P = 128
S = 512
H = 2048
HD = 128
HALF = 64
NH = 16
NKV = 4
THETA = 10000.0
TT = S // P
PASSES = H // 512
UNIT = 512
RT = UNIT // P
WORDS = H // 2

FLOPS = 2 * S * H * (NH + 2 * NKV) * HD

S_ROWS = 4
ROWS_BUFS = 10


def tile_efficientattention_pa_kernel(tc, x, Wq_bytes, Wq_scale, Wk, Wv, out_0, out_1, out_2):
    nc = tc.nc
    x_rows = x.rearrange("b s h -> (b s) h")
    q_out = out_0.rearrange("b h s d -> (b h) s d")
    k_out = out_1.rearrange("b h s d -> (b h) s d")
    v_out = out_2.rearrange("b h s d -> (b h) s d")

    with ExitStack() as ctx:
        const = ctx.enter_context(tc.tile_pool(name="const", bufs=1))
        src = ctx.enter_context(tc.tile_pool(name="src", bufs=1))
        work = ctx.enter_context(tc.tile_pool(name="work", bufs=2))
        ps_t = ctx.enter_context(tc.psum_pool(name="ps_t", bufs=4))
        ps_a = ctx.enter_context(tc.psum_pool(name="ps_a", bufs=4))
        ctx.enter_context(tc.manual_schedule())

        wq_bytes_sb = []
        for rt in range(NH):
            wq_bytes_sb.append(src.tile([P, H], U8, name="wq_bytes_%d" % rt))
        scale_bc = src.tile([P, H], F32, name="scale_bc")
        scale_col = src.tile([P, PASSES, 4], F32, name="scale_col")

        def load_q(rt):
            nc.sync.dma_start(out=wq_bytes_sb[rt][:], in_=Wq_bytes[rt * P:(rt + 1) * P, :])

        def load_rows(dram, i):
            rows = src.tile([P, H], BF16, name="rows", tag="rows", bufs=ROWS_BUFS)
            nc.sync.dma_start(out=rows[:], in_=dram[i * P:(i + 1) * P, :])
            return rows

        nc.scalar.dma_start(out=scale_col[:], in_=Wq_scale.rearrange("o (g p t) -> p (o g) t", p=P, t=4))
        for rt in range(0, 4):
            load_q(rt)
        for rt in range(12, 14):
            load_q(rt)
        nc.sync.dma_start(out=scale_bc[:], in_=Wq_scale.rearrange("o k -> (o k)").partition_broadcast(P))
        for rt in range(4, 6):
            load_q(rt)
        early = []
        for rt in range(RT):
            rows = src.tile([P, H], BF16, name="rows", tag="rows", bufs=ROWS_BUFS)
            early.append(rows)
        x_sb = [load_rows(x_rows, i) for i in range(TT)]
        for rt in range(6, 8):
            load_q(rt)

        pos = const.tile([P, TT], F32, name="pos")
        nc.gpsimd.iota(pos[:], pattern=[[P, TT]], base=0, channel_multiplier=1, allow_small_or_imprecise_dtypes=True)
        ident = const.tile([P, P], F32, name="ident")
        make_identity(nc, ident[:])
        casts = []
        for rt in range(12, 14):
            rows = src.tile([P, H], BF16, name="cast_%d" % rt)
            nc.gpsimd.tensor_copy(out=rows[:], in_=wq_bytes_sb[rt][:].bitcast(FP8))
            casts.append(rows)
        ang = work.tile([P, 2, TT, HALF], F32, name="ang", tag="ta", bufs=6)
        turns = work.tile([P, 2, TT, HALF], I32, name="turns", tag="ta", bufs=6)
        whole = work.tile([P, 2, TT, HALF], F32, name="whole", tag="ta", bufs=6)
        nc.vector.tensor_scalar(out=ang[:, 0, :, 0], in0=pos[:], scalar1=1.0 / (2.0 * math.pi), scalar2=None, op0=ALU.mult)
        for b in range(6):
            w = 1 << b
            nc.vector.tensor_scalar(out=ang[:, 0, :, w:2 * w], in0=ang[:, 0, :, 0:w], scalar1=THETA ** (-w / HALF),
                                    scalar2=None, op0=ALU.mult)
        nc.vector.tensor_scalar(out=ang[:, 1], in0=ang[:, 0], scalar1=0.25, scalar2=None, op0=ALU.add)
        nc.vector.tensor_copy(out=turns[:], in_=ang[:])
        nc.vector.tensor_copy(out=whole[:], in_=turns[:])
        nc.vector.tensor_tensor(out=ang[:], in0=ang[:], in1=whole[:], op=ALU.subtract)
        cos1 = const.tile([P, TT, HALF], F32, name="cos1")
        sin_rot = const.tile([P, TT, 2, HALF], F32, name="sin_rot")

        x_codes = const.tile([P, TT, UNIT], U32, name="x_codes", align_bytes=64)
        x_scales = const.tile([P, TT, UNIT], U8, name="x_scales", align_bytes=64)

        def widen(rt, pieces=1):
            wb = work.tile([P, H], BF16, name="wb", tag="wb", bufs=5)
            w = H // pieces
            for c in range(pieces):
                nc.vector.tensor_tensor(out=wb[:, c * w:(c + 1) * w], in0=wq_bytes_sb[rt][:, c * w:(c + 1) * w].bitcast(FP8),
                                        in1=scale_bc[:, c * w:(c + 1) * w], op=ALU.mult)
            return wb

        def new_grouped():
            return work.tile([P, 4, UNIT, 2], F32, name="grouped", tag="grouped", bufs=3, align_bytes=64)

        def transpose_rows(rows_bf16, dst_of_pair):
            words = rows_bf16[:].bitcast(F32)
            for gp in range(2):
                tb = ps_t.tile([P, 2, 2, P], F32, name="tb", tag="tb", bufs=4)
                for gg in range(2):
                    g = 2 * gp + gg
                    for u in range(2):
                        nc.tensor.transpose(tb[:, gg, u, :], words[:, 256 * g + u:256 * (g + 1):2], ident[:])
                nc.scalar.copy(out=dst_of_pair(gp), in_=tb[:].rearrange("p g u r -> p g r u"))

        def transpose_x(grouped, i):
            transpose_rows(x_sb[i], lambda gp: grouped[:, i, 256 * gp:256 * (gp + 1), :].rearrange(
                "p (g r) u -> p g r u", g=2))

        def transpose_w(grouped, rows_bf16, rt):
            transpose_rows(rows_bf16, lambda gp: grouped[:, 2 * gp:2 * gp + 2, rt * P:(rt + 1) * P, :])

        def cast_rows(rt):
            rows = src.tile([P, H], BF16, name="rows", tag="rows", bufs=ROWS_BUFS)
            nc.scalar.copy(out=rows[:], in_=wq_bytes_sb[rt][:].bitcast(FP8))
            return rows

        def cast_early(rt, pieces):
            n = H // pieces
            for c in range(pieces):
                nc.scalar.copy(out=early[rt][:, c * n:(c + 1) * n], in_=wq_bytes_sb[rt][:, c * n:(c + 1) * n].bitcast(FP8))

        def transpose_product(grouped, rows_bf16, rt):
            words = rows_bf16[:].bitcast(F32)
            for gp in range(2):
                tb = ps_t.tile([P, 2, 2, P], F32, name="tb", tag="tb", bufs=4)
                for gg in range(2):
                    g = 2 * gp + gg
                    for u in range(2):
                        nc.tensor.transpose(tb[:, gg, u, :], words[:, 256 * g + u:256 * (g + 1):2], ident[:])
                for gg in range(2):
                    g = 2 * gp + gg
                    nc.vector.tensor_tensor(
                        out=grouped[:, g, rt * P:(rt + 1) * P, :].rearrange("p r u -> p (r u)").bitcast(BF16).rearrange("p (r u e) -> p r u e", u=2, e=2),
                        in0=tb[:, gg].rearrange("p u r -> p (u r)").bitcast(BF16).rearrange("p (u r e) -> p r u e", u=2, e=2),
                        in1=scale_col[:, g:g + 1, :].to_broadcast([P, P, 4]).rearrange("p r (u e) -> p r u e", u=2),
                        op=ALU.mult)

        def new_planes():
            return work.tile([P, 4, UNIT], BF16, name="planes", tag="planes", bufs=2)

        def scaled_planes(planes, g, u):
            tb = ps_t.tile([P, S_ROWS * P], F32, name="tb", tag="tb", bufs=4)
            for rt in range(S_ROWS):
                nc.tensor.transpose(tb[:, rt * P:(rt + 1) * P], casts[rt][:].bitcast(F32)[:, 256 * g + u:256 * (g + 1):2],
                                    ident[:])
            halves = tb[:].bitcast(BF16).rearrange("p (n e) -> p n e", e=2)
            for e in range(2):
                t = 2 * u + e
                nc.scalar.activation(out=planes[:, t, :], in_=halves[:, :, e], func=ACT.Copy,
                                     scale=scale_col[:, g, t:t + 1])

        def interleave(planes, grouped, g):
            dst = grouped[:, g].rearrange("p n u -> p (n u)").bitcast(BF16).rearrange("p (n t) -> p n t", t=4)
            nc.scalar.copy(out=dst, in_=planes[:].rearrange("p t n -> p n t"))

        def scaled_pass(grouped, g):
            planes = new_planes()
            scaled_planes(planes, g, 0)
            scaled_planes(planes, g, 1)
            return planes

        def quantize(grouped, codes, scales):
            for a in range(2):
                nc.vector.quantize_mx(
                    out=codes[:, 2 * a:2 * a + 2, :].rearrange("p g n -> p (g n)").bitcast(FP8X4),
                    scales=scales[:, 2 * a:2 * a + 2, :].rearrange("p g n -> p (g n)"),
                    in_=grouped[:, 2 * a:2 * a + 2].rearrange("p g n u -> p (g n u)").bitcast(BF16),
                )

        v_codes = const.tile([P, PASSES, UNIT], U32, name="v_codes", align_bytes=64)
        v_scales = const.tile([P, PASSES, UNIT], U8, name="v_scales", align_bytes=64)

        def quantize_unit(grouped):
            codes = work.tile([P, PASSES, UNIT], U32, name="w_codes", tag="w_codes", bufs=2, align_bytes=64)
            scales = work.tile([P, PASSES, UNIT], U8, name="w_scales", tag="w_scales", bufs=2, align_bytes=64)
            quantize(grouped, codes, scales)
            return codes, scales

        def project_tile(unit_codes, i, pool=None, tag="acc"):
            codes, scales = unit_codes
            acc = (pool or ps_a).tile([P, 4, HD], F32, name="acc", tag=tag, bufs=4)
            for g in range(PASSES):
                nc.tensor.matmul_mx(
                    out=acc[:].rearrange("p h d -> p (h d)"),
                    lhsT=x_codes[:, i, g * P:(g + 1) * P].bitcast(FP8X4),
                    lhsT_scale=x_scales[:, i, g * P:(g + 1) * P],
                    rhs=codes[:, g, :].bitcast(FP8X4),
                    rhs_scale=scales[:, g, :],
                    start=(g == 0),
                    stop=(g == PASSES - 1),
                )
            return acc

        def cos_product(acc, i):
            ta = work.tile([P, 4, HD], F32, name="ta", tag="ta", bufs=6)
            nc.vector.tensor_tensor(out=ta[:].rearrange("p h (c j) -> p (h c) j", c=2),
                                    in0=acc[:].rearrange("p h (c j) -> p (h c) j", c=2),
                                    in1=cos1[:, i:i + 1, :].to_broadcast([P, 8, HALF]), op=ALU.mult)
            return ta

        def sin_product(acc, i):
            ts = work.tile([P, 4, HD], F32, name="ts", tag="ts", bufs=4)
            nc.vector.tensor_tensor(out=ts[:].rearrange("p h (c j) -> p h c j", c=2),
                                    in0=acc[:].rearrange("p h (c j) -> p h c j", c=2)[:, :, ::-1, :],
                                    in1=sin_rot[:, i:i + 1, :, :].to_broadcast([P, 4, 2, HALF]), op=ALU.mult)
            return ts

        def add_and_store(engine, ta, ts, dram, i):
            engine.tensor_tensor(out=ta[:], in0=ta[:], in1=ts[:], op=ALU.add)
            nc.sync.dma_start(out=dram[:, i * P:(i + 1) * P, :].rearrange("h p d -> p h d"), in_=ta[:])

        def finish(carried):
            acc3, ta3, dram3 = carried
            add_and_store(nc.gpsimd, ta3, sin_product(acc3, 3), dram3, 3)

        def rope(accs, dram, last=False):
            kept = None
            for i in range(3):
                ta = cos_product(accs[i], i)
                ts = sin_product(accs[i], i)
                if i < 2:
                    add_and_store(nc.gpsimd, ta, ts, dram, i)
                else:
                    kept = (ta, ts)
            ta3 = cos_product(accs[3], 3)
            if last:
                ts3 = sin_product(accs[3], 3)
                add_and_store(nc.vector, kept[0], kept[1], dram, 2)
                for h in range(0, 4, 2):
                    nc.vector.tensor_tensor(out=ta3[:, h:h + 2], in0=ta3[:, h:h + 2], in1=ts3[:, h:h + 2], op=ALU.add)
                    nc.sync.dma_start(out=dram[h:h + 2, 3 * P:4 * P, :].rearrange("h p d -> p h d"), in_=ta3[:, h:h + 2])
                return None
            add_and_store(nc.vector, kept[0], kept[1], dram, 2)
            return (accs[3], ta3, dram)

        def copy_out(accs, dram):
            for i in range(TT):
                vt = work.tile([P, 4, HD], F32, name="vt", tag="vt", bufs=3)
                nc.scalar.copy(out=vt[:], in_=accs[i][:])
                nc.scalar.dma_start(out=dram[:, i * P:(i + 1) * P, :].rearrange("h p d -> p h d"), in_=vt[:])

        for rt in range(RT):
            cast_early(rt, 2)
        nc.scalar.activation(out=cos1[:], in_=ang[:, 1], func=ACT.Sin, scale=2.0 * math.pi)
        nc.scalar.activation(out=sin_rot[:, :, 0, :], in_=ang[:, 0], func=ACT.Sin, scale=-2.0 * math.pi)
        nc.scalar.activation(out=sin_rot[:, :, 1, :], in_=ang[:, 0], func=ACT.Sin, scale=2.0 * math.pi)
        g_x = new_grouped()
        g_q0 = new_grouped()
        for rt in range(RT):
            transpose_product(g_q0, early[rt], rt)
        for i in range(TT):
            transpose_x(g_x, i)
        wv_sb = [load_rows(Wv, i) for i in range(TT)]
        for rt in range(14, 16):
            load_q(rt)
        for rt in range(8, 12):
            load_q(rt)
        wide1 = [widen(4 + rt) for rt in range(2)]
        quantize(g_x, x_codes, x_scales)
        g_v = new_grouped()
        for rt in range(RT):
            transpose_w(g_v, wv_sb[rt], rt)
        c_q0 = quantize_unit(g_q0)
        a_q0 = [project_tile(c_q0, i) for i in range(TT)]
        wk_sb = [load_rows(Wk, i) for i in range(TT)]
        for rt in range(2):
            casts.append(cast_rows(14 + rt))
        g_q1 = new_grouped()
        for rt in range(RT):
            transpose_w(g_q1, wide1[rt] if rt < 2 else widen(4 + rt), rt)
        quantize(g_v, v_codes, v_scales)
        g_q2 = new_grouped()
        g_q3 = new_grouped()
        planes0 = scaled_pass(g_q3, 0)
        transpose_w(g_q2, widen(8), 0)
        transpose_w(g_q2, widen(9), 1)
        transpose_w(g_q2, widen(10), 2)
        transpose_w(g_q2, widen(11), 3)
        c_q1 = quantize_unit(g_q1)
        g_k = new_grouped()
        carried = rope(a_q0, q_out[0:4])
        a_q1 = []
        transpose_w(g_k, wk_sb[0], 0)
        transpose_w(g_k, wk_sb[1], 1)
        transpose_w(g_k, wk_sb[2], 2)
        transpose_w(g_k, wk_sb[3], 3)
        planes1 = scaled_pass(g_q3, 1)
        a_q1.append(project_tile(c_q1, 0))
        a_q1.append(project_tile(c_q1, 1))
        a_q1.append(project_tile(c_q1, 2))
        c_q2 = quantize_unit(g_q2)
        finish(carried)
        a_q1.append(project_tile(c_q1, 3))
        interleave(planes0, g_q3, 0)
        interleave(planes1, g_q3, 1)
        planes2 = scaled_pass(g_q3, 2)
        carried = rope(a_q1, q_out[4:8])
        planes3 = scaled_pass(g_q3, 3)
        interleave(planes2, g_q3, 2)
        interleave(planes3, g_q3, 3)
        a_q2 = [project_tile(c_q2, i) for i in range(3)]
        c_k = quantize_unit(g_k)
        finish(carried)
        a_q2.append(project_tile(c_q2, 3))
        carried = rope(a_q2, q_out[8:12])
        a_v = [project_tile((v_codes, v_scales), i, ps_t, "tb") for i in range(1)]
        a_k = [project_tile(c_k, i) for i in range(3)]
        finish(carried)
        a_k.append(project_tile(c_k, 3))
        a_v += [project_tile((v_codes, v_scales), i, ps_t, "tb") for i in range(1, TT)]
        carried = rope(a_k, k_out)
        c_q3 = quantize_unit(g_q3)
        a_q3 = [project_tile(c_q3, i) for i in range(3)]
        copy_out(a_v, v_out)
        finish(carried)
        a_q3.append(project_tile(c_q3, 3))
        rope(a_q3, q_out[12:16], last=True)
